import numpy as np
import ml_dtypes


def mxq(x, axis, fmt="e4m3"):
    dtype, down = {"e4m3": (ml_dtypes.float8_e4m3fn, 7), "e5m2": (ml_dtypes.float8_e5m2, 14)}[fmt]
    v = np.moveaxis(np.asarray(x, np.float32).astype(ml_dtypes.bfloat16).astype(np.float64), axis, -1)
    blocks = v.reshape(v.shape[:-1] + (-1, 32))
    amax = np.abs(blocks).max(-1, keepdims=True)
    byte = np.maximum(np.where(amax > 0, np.frexp(amax)[1] - 1 + 127, 0) - down, 1)
    scale = np.exp2(byte - 127.0)
    codes = (blocks / scale).astype(np.float32).astype(dtype).astype(np.float64)
    return np.moveaxis((codes * scale).reshape(v.shape), -1, axis)


WIDE = False


def mx_kscale(k):
    if not WIDE:
        return np.ones(k)
    levels = np.array([10, -10, 5, -5, 0])
    if k % 512:
        return np.exp2(np.random.permutation(np.resize(levels, k // 32))).repeat(32)
    a = np.empty((k // 512, 16))
    for p in range(k // 512):
        a[p, :8] = np.random.permutation(np.resize(levels, 8))
        for g in range(8):
            far = levels[np.abs(levels - a[p, g]) >= 10]
            a[p, g + 8] = far[np.random.randint(len(far))]
    return np.exp2(a.ravel()).repeat(32)


BF16 = ml_dtypes.bfloat16


def bf(x):
    return np.asarray(x, np.float32).astype(BF16)


def f64(x):
    return np.asarray(x).astype(np.float64)


B, IM, HID, L = 1024, 1024, 4096, 128


def relu(v):
    return np.maximum(v, 0.0)


def draw0():
    s, t = mx_kscale(IM), mx_kscale(HID)
    return {"x": bf(np.random.random((B, IM)) * s),
            "eps": bf(np.random.standard_normal((B, L))),
            "W11": bf(np.random.standard_normal((IM, HID)) * np.sqrt(3.0 / IM) / s[:, None] * t),
            "b11": bf(np.random.standard_normal(HID) * 0.2 * t),
            "W31": bf(np.random.standard_normal((HID, L)) * np.sqrt(2.0 / HID) / t[:, None]),
            "b31": bf(np.random.standard_normal(L) * 0.2),
            "W32": bf(np.random.standard_normal((HID, L)) * np.sqrt(2.0 / HID) / t[:, None]),
            "b32": bf(np.random.standard_normal(L) * 0.2)}


def core(x, eps, W11, b11, W31, b31, W32, b32):
    enc = relu((mxq(f64(x), 1, "e4m3") @ mxq(f64(W11), 0, "e4m3")) + f64(b11))
    encq = mxq(enc, 1, "e4m3")
    mu = relu((encq @ mxq(f64(W31), 0, "e4m3")) + f64(b31))
    sigma = relu((encq @ mxq(f64(W32), 0, "e4m3")) + f64(b32))
    z = f64(eps) * sigma + mu
    return mu, sigma, z


def e4m3fn_bytes(y):
    return np.clip(np.asarray(y, np.float64), -448.0, 448.0).astype(np.float32).astype(ml_dtypes.float8_e4m3fn).view(np.uint8)


def e4m3fn_values(b):
    return np.asarray(b, np.uint8).view(ml_dtypes.float8_e4m3fn).astype(np.float64)


def setup_inputs():
    d = draw0()
    x0 = np.asarray(d['x']).astype(np.float64)
    s = (np.max(np.abs(x0), axis=(0,), keepdims=True) / 448.0).astype(np.float32)
    out = {}
    for k, v in d.items():
        if k == 'x':
            out['x_bytes'] = e4m3fn_bytes(x0 / s.astype(np.float64))
            out['x_scale'] = s
        else:
            out[k] = v
    return out


def reference(x_bytes, x_scale, eps, W11, b11, W31, b31, W32, b32):
    return core(e4m3fn_values(x_bytes) * x_scale.astype(np.float64), eps, W11, b11, W31, b31, W32, b32)

@@ -1,0 +1,377 @@
+from contextlib import ExitStack
+
+import concourse.mybir as mybir
+from concourse.masks import make_identity
+
+TOKENS, IMAGE, HIDDEN, LATENT = 1024, 1024, 4096, 128
+
+F32 = mybir.dt.float32
+BF16 = mybir.dt.bfloat16
+U32 = mybir.dt.uint32
+U8 = mybir.dt.uint8
+FP8 = mybir.dt.float8_e4m3fn
+FP8X4 = mybir.dt.float8_e4m3fn_x4
+
+ADD = mybir.AluOpType.add
+MULT = mybir.AluOpType.mult
+MAX = mybir.AluOpType.max
+RELU = mybir.ActivationFunctionType.Relu
+
+P = 128
+FLOPS = 2 * TOKENS * IMAGE * HIDDEN + 2 * TOKENS * HIDDEN * 2 * LATENT
+
+GROUPS = 8
+HALF = 512
+ROWS = TOKENS // P
+SCALAR_PIECES = 2
+
+UNITS = [(0, 0)] + [(h, g - h) for g in range(1, GROUPS) for h in range(2)] + [(1, GROUPS - 1)]
+
+
+def tile_mae_pa_kernel(tc, x_bytes, x_scale, eps, W11, b11, W31, b31, W32, b32, out_0, out_1, out_2):
+    nc = tc.nc
+    with ExitStack() as ctx:
+        keep = ctx.enter_context(tc.tile_pool(name="keep", bufs=1))
+        work = ctx.enter_context(tc.tile_pool(name="work", bufs=2))
+        psum = ctx.enter_context(tc.psum_pool(name="psum", bufs=4))
+        accs = ctx.enter_context(tc.psum_pool(name="accs", bufs=1))
+
+        ident = keep.tile([P, P], F32, name="ident")
+        make_identity(nc, ident[:])
+        ctx.enter_context(tc.manual_schedule())
+        ctx.enter_context(nc.allow_non_contiguous_dma(reason="runs of four biases"))
+
+        warm = keep.tile([P, 1], F32, name="warm")
+        nc.vector.memset(warm[:], 0.0)
+        warm_out = keep.tile([P, 1], F32, name="warm_out")
+
+        scale = keep.tile([P, IMAGE], F32, name="scale")
+        nc.scalar.dma_start(out=scale[:], in_=x_scale.rearrange("o k -> (o k)").partition_broadcast(P))
+        nc.scalar.activation(out=warm_out[:], in_=warm[:], func=RELU)
+
+        xq = [keep.tile([P, 4 * IMAGE], U8, name=f"xq{h}") for h in range(2)]
+        x_view = x_bytes.rearrange("(p r) k -> p (r k)", r=ROWS)
+
+        def load_x(h, a, b):
+            nc.sync.dma_start(
+                out=xq[h][:, a * IMAGE : b * IMAGE],
+                in_=x_view[:, (4 * h + a) * IMAGE : (4 * h + b) * IMAGE],
+            )
+
+        w_raw = [None] * 4
+        w_view = W11.rearrange("(c p j) n -> c p j n", c=2, j=4)
+
+        def load_w(pair, c, a, b):
+            if w_raw[pair] is None:
+                w_raw[pair] = work.tile([P, 2, 4, 1024], BF16, name="w_raw", bufs=3)
+            nc.sync.dma_start(
+                out=w_raw[pair][:, c, :, a:b], in_=w_view[c, :, :, 1024 * pair + a : 1024 * pair + b]
+            )
+
+        w3_raw = [keep.tile([P, GROUPS, 512], BF16, name=f"w3_raw{i}") for i in range(2)]
+        w3_view = [w.rearrange("(g p j) l -> p g (j l)", p=P, j=4) for w in (W31, W32)]
+
+        def load_w3(a, b):
+            for i in range(2):
+                nc.sync.dma_start(out=w3_raw[i][:, a:b, :], in_=w3_view[i][:, a:b, :])
+
+        load_x(0, 0, 2)
+        load_x(0, 2, 4)
+        load_w(0, 0, 0, 512)
+        load_w(0, 1, 0, 512)
+        bias_raw = keep.tile([P, GROUPS, 4], BF16, name="bias_raw")
+        nc.scalar.dma_start(out=bias_raw[:], in_=b11.rearrange("(g p t) -> p g t", p=P, t=4))
+        load_x(1, 0, 4)
+        load_w(0, 0, 512, 1024)
+        load_w(0, 1, 512, 1024)
+        load_w3(0, 2)
+        load_w(1, 0, 0, 1024)
+        load_w(1, 1, 0, 1024)
+        load_w3(2, 8)
+        bias3 = keep.tile([P, 2 * LATENT], BF16, name="bias3")
+        nc.sync.dma_start(out=bias3[:, :LATENT], in_=b31.partition_broadcast(P))
+        nc.sync.dma_start(out=bias3[:, LATENT:], in_=b32.partition_broadcast(P))
+        eps_sb = keep.tile([P, ROWS, LATENT], BF16, name="eps_sb")
+        nc.sync.dma_start(out=eps_sb[:], in_=eps.rearrange("(p r) l -> p r l", r=ROWS))
+        load_w(2, 0, 0, 1024)
+        load_w(2, 1, 0, 1024)
+
+        xg = [None, None]
+        x_codes = [keep.tile([P, 2, HALF], U32, name=f"x_codes{h}", align_bytes=64) for h in range(2)]
+        x_planes = [keep.tile([P, 2, HALF], U8, name=f"x_planes{h}", align_bytes=64) for h in range(2)]
+
+        xb = {}
+
+        def x_product(h, r):
+            xb[h, r] = work.tile([P, IMAGE], BF16, name="xb", bufs=3)
+            nc.vector.tensor_tensor(
+                out=xb[h, r][:], in0=xq[h][:, r * IMAGE : (r + 1) * IMAGE].bitcast(FP8), in1=scale[:], op=MULT
+            )
+
+        x_banks = {}
+
+        def x_turn(h, r):
+            bank = psum.tile([P, 4, P], F32, name="bank")
+            words = xb[h, r][:].bitcast(F32)
+            for c in range(2):
+                for u in range(2):
+                    nc.tensor.transpose(
+                        bank[:, 2 * c + u, :], words[:, 256 * c + u : 256 * (c + 1) : 2], ident[:]
+                    )
+            x_banks[h, r] = bank
+
+        def x_out(h, r):
+            if xg[h] is None:
+                xg[h] = work.tile([P, 2, HALF, 4], BF16, name="xg", bufs=2, align_bytes=64)
+            dst = xg[h][:].rearrange("p c n t -> p (c n t)").bitcast(F32)
+            dst = dst.rearrange("p (c n u) -> p c n u", c=2, u=2)
+            nc.scalar.copy(
+                out=dst[:, :, P * r : P * (r + 1), :],
+                in_=x_banks[h, r][:].rearrange("p (c u) n -> p c n u", u=2),
+            )
+
+        def x_quant(h, c):
+            nc.vector.quantize_mx(
+                out=x_codes[h][:, c, :].bitcast(FP8X4),
+                scales=x_planes[h][:, c, :],
+                in_=xg[h][:, c, :, :].rearrange("p n t -> p (n t)"),
+            )
+
+        wg, w_codes, w_planes = {}, {}, {}
+
+        def w_piece(engine_copy, g, c, m):
+            if (g, c) not in wg:
+                wg[g, c] = work.tile([P, 2048], BF16, name="wg", bufs=4, align_bytes=64)
+            off = 512 * (g % 2) + 128 * m
+            engine_copy(
+                out=wg[g, c][:].rearrange("p (t m j) -> p m j t", t=4, j=4)[:, 32 * m : 32 * (m + 1), :, :],
+                in_=w_raw[g // 2][:, c, :, off : off + 128].rearrange("p j (m t) -> p m j t", t=4),
+            )
+
+        def w_scalar(g, c, m):
+            w_piece(nc.scalar.copy, g, c, m)
+
+        def w_vector(g, c, m):
+            w_piece(nc.vector.tensor_copy, g, c, m)
+
+        def w_quant(g, c):
+            if g not in w_codes:
+                w_codes[g] = work.tile([P, 2, 512], U32, name="w_codes", bufs=4, align_bytes=64)
+                w_planes[g] = work.tile([P, 2, 512], U8, name="w_planes", bufs=4, align_bytes=64)
+            nc.vector.quantize_mx(
+                out=w_codes[g][:, c, :].bitcast(FP8X4), scales=w_planes[g][:, c, :], in_=wg[g, c][:]
+            )
+
+        w3g = {}
+        w3_codes = keep.tile([P, GROUPS, 2 * LATENT], U32, name="w3_codes", align_bytes=64)
+        w3_planes = keep.tile([P, GROUPS, 2 * LATENT], U8, name="w3_planes", align_bytes=64)
+
+        def w3_lay(g):
+            w3g[g] = work.tile([P, 1024], BF16, name="w3g", bufs=2, align_bytes=64)
+            for i in range(2):
+                nc.vector.tensor_copy(
+                    out=w3g[g][:, 512 * i : 512 * (i + 1)].rearrange("p (c i j) -> p c j i", i=4, j=4),
+                    in_=w3_raw[i][:, g, :].rearrange("p (j c i) -> p c j i", j=4, i=4),
+                )
+
+        def w3_quant(g):
+            nc.vector.quantize_mx(
+                out=w3_codes[:, g, :].bitcast(FP8X4), scales=w3_planes[:, g, :], in_=w3g[g][:]
+            )
+
+        bias = keep.tile([P, GROUPS, 4], F32, name="bias")
+        enc, encg, enc_codes, enc_planes = {}, {}, {}, {}
+
+        def first_stage(h, g, between):
+            enc[h, g] = work.tile([P, 4, HALF], BF16, name="enc", bufs=3)
+            for t in range(4):
+                bank = psum.tile([P, 4, P], F32, name="bank")
+                flat = bank[:].rearrange("p a b -> p (a b)")
+                for c in range(2):
+                    nc.tensor.matmul_mx(
+                        out=flat,
+                        lhsT=w_codes[g][:, c, P * t : P * (t + 1)].bitcast(FP8X4),
+                        lhsT_scale=w_planes[g][:, c, P * t : P * (t + 1)],
+                        rhs=x_codes[h][:, c, :].bitcast(FP8X4),
+                        rhs_scale=x_planes[h][:, c, :],
+                        start=(c == 0),
+                        stop=(c == 1),
+                    )
+                nc.scalar.activation(out=enc[h, g][:, t, :], in_=flat, func=RELU, bias=bias[:, g, t : t + 1])
+                for call in between[t : t + 1]:
+                    for args in call:
+                        w_scalar(*args)
+
+        def enc_lay(h, g, a=0, b=HALF):
+            if (h, g) not in encg:
+                encg[h, g] = work.tile([P, 4 * HALF], BF16, name="encg", bufs=3, align_bytes=64)
+            nc.vector.tensor_copy(
+                out=encg[h, g][:, 4 * a : 4 * b].rearrange("p (c i t) -> p c t i", i=4, t=4),
+                in_=enc[h, g][:, :, a:b].rearrange("p t (c i) -> p c t i", i=4),
+            )
+
+        def enc_quant(h, g, a=0, b=HALF):
+            if (h, g) not in enc_codes:
+                bufs = 3 if h == 0 else 8
+                enc_codes[h, g] = work.tile([P, HALF], U32, name=f"enc_codes{h}", bufs=bufs, align_bytes=64)
+                enc_planes[h, g] = work.tile([P, HALF], U8, name=f"enc_planes{h}", bufs=bufs, align_bytes=64)
+            nc.vector.quantize_mx(
+                out=enc_codes[h, g][:, a:b].bitcast(FP8X4),
+                scales=enc_planes[h, g][:, a:b],
+                in_=encg[h, g][:, 4 * a : 4 * b],
+            )
+
+        acc = {}
+
+        def second_stage(h, g, rows=(0, 1, 2, 3)):
+            for r in rows:
+                if (h, r) not in acc:
+                    acc[h, r] = accs.tile([P, 2 * LATENT], F32, name=f"acc{r}")
+                nc.tensor.matmul_mx(
+                    out=acc[h, r][:],
+                    lhsT=enc_codes[h, g][:, P * r : P * (r + 1)].bitcast(FP8X4),
+                    lhsT_scale=enc_planes[h, g][:, P * r : P * (r + 1)],
+                    rhs=w3_codes[:, g, :].bitcast(FP8X4),
+                    rhs_scale=w3_planes[:, g, :],
+                    start=(g == 0),
+                    stop=(g == GROUPS - 1),
+                )
+
+        y, z, relus = {}, {}, {}
+        views = [o.rearrange("(p r) l -> p r l", r=ROWS) for o in (out_0, out_1, out_2)]
+
+        def add_bias(h, r):
+            if h not in y:
+                y[h] = work.tile([P, 4, 2 * LATENT], F32, name="y", bufs=2)
+                z[h] = work.tile([P, 4, LATENT], F32, name="z", bufs=2)
+                relus[h] = [work.tile([P, 4, LATENT], F32, name=f"relu{i}", bufs=2) for i in range(2)]
+            nc.vector.tensor_tensor(out=y[h][:, r, :], in0=acc[h, r][:], in1=bias3[:], op=ADD)
+
+        def relu_out(h, i, a, b):
+            nc.scalar.activation(
+                out=relus[h][i][:, a:b, :], in_=y[h][:, a:b, LATENT * i : LATENT * (i + 1)], func=RELU
+            )
+            nc.sync.dma_start(out=views[i][:, 4 * h + a : 4 * h + b, :], in_=relus[h][i][:, a:b, :])
+
+        def z_noise(h, a, b):
+            nc.vector.scalar_tensor_tensor(
+                out=z[h][:, a:b, :], in0=y[h][:, a:b, LATENT:], scalar=0.0,
+                in1=eps_sb[:, 4 * h + a : 4 * h + b, :], op0=MAX, op1=MULT,
+            )
+
+        def z_out(h, a, b):
+            nc.vector.scalar_tensor_tensor(
+                out=z[h][:, a:b, :], in0=y[h][:, a:b, :LATENT], scalar=0.0,
+                in1=z[h][:, a:b, :], op0=MAX, op1=ADD,
+            )
+            nc.sync.dma_start(out=views[2][:, 4 * h + a : 4 * h + b, :], in_=z[h][:, a:b, :])
+
+        for r in range(4):
+            x_product(0, r)
+            x_turn(0, r)
+            x_out(0, r)
+            w_scalar(0, 0, r)
+        w_scalar(0, 1, 0)
+        nc.vector.tensor_copy(out=bias[:], in_=bias_raw[:])
+        for m in (1, 2, 3):
+            w_vector(0, 1, m)
+        x_quant(0, 0)
+        x_quant(0, 1)
+        w_quant(0, 0)
+        w_quant(0, 1)
+        w_scalar(1, 0, 0)
+        w_scalar(1, 0, 1)
+
+        first_stage(0, 0, [[(1, 0, 2)], [(1, 0, 3)], [(1, 1, 0)], [(1, 1, 1)]])
+        x_product(1, 0)
+        x_turn(1, 0)
+        x_out(1, 0)
+        x_product(1, 1)
+        x_turn(1, 1)
+        x_out(1, 1)
+        w_scalar(1, 1, 2)
+        w_scalar(1, 1, 3)
+        w3_lay(0)
+        enc_lay(0, 0)
+        x_product(1, 2)
+        x_turn(1, 2)
+        x_out(1, 2)
+        w_quant(1, 0)
+        enc_quant(0, 0)
+        x_product(1, 3)
+        x_turn(1, 3)
+        x_out(1, 3)
+        w3_quant(0)
+        w_quant(1, 1)
+
+        first_stage(0, 1, [[(2, 0, 0)], [(2, 0, 1)], [(2, 1, 0)], [(2, 1, 1)]])
+        second_stage(0, 0)
+        w_vector(2, 0, 2)
+        w_vector(2, 0, 3)
+        x_quant(1, 0)
+        x_quant(1, 1)
+        w3_lay(1)
+        enc_lay(0, 1)
+        w_vector(2, 1, 2)
+        w_vector(2, 1, 3)
+        w3_quant(1)
+        enc_quant(0, 1)
+        w_quant(2, 0)
+
+        load_w(3, 0, 0, 1024)
+        load_w(3, 1, 0, 1024)
+
+        for step in range(2, 16):
+            h, g = UNITS[step]
+            pg, pc = (step + 4) // 2, step % 2
+            prep = pg < GROUPS
+            scalar_calls = [[], [], [], []]
+            if prep:
+                for m in range(SCALAR_PIECES):
+                    scalar_calls[2 * m + 1 if SCALAR_PIECES == 2 else m].append((pg, pc, m))
+            first_stage(h, g, scalar_calls)
+            ph, pgrp = UNITS[step - 1]
+            if ph == 0:
+                second_stage(ph, pgrp)
+            if step == 15:
+                for gg in range(GROUPS - 1):
+                    second_stage(1, gg)
+                z_noise(0, 0, 4)
+                z_out(0, 0, 4)
+                relu_out(0, 0, 0, 4)
+                relu_out(0, 1, 0, 4)
+                enc_lay(h, g, 0, 256)
+                enc_lay(h, g, 256, 512)
+                enc_quant(h, g, 0, 256)
+                enc_quant(h, g, 256, 512)
+                break
+            qg, qc = (step + 3) // 2, (step - 1) % 2
+            if qg < GROUPS:
+                w_quant(qg, qc)
+            if prep:
+                for m in range(SCALAR_PIECES, 4):
+                    w_vector(pg, pc, m)
+            w3_group = (step + 2) // 2 if step % 2 == 0 else (step + 1) // 2
+            enc_lay(h, g)
+            if w3_group < GROUPS:
+                if step % 2 == 0:
+                    w3_lay(w3_group)
+                else:
+                    w3_quant(w3_group)
+            if step == 14:
+                add_bias(0, 0)
+                add_bias(0, 1)
+            enc_quant(h, g)
+            if step == 14:
+                add_bias(0, 2)
+                add_bias(0, 3)
+
+        for a in (0, 2):
+            second_stage(1, GROUPS - 1, rows=(a, a + 1))
+        for a in (0, 2):
+            add_bias(1, a)
+            add_bias(1, a + 1)
+            relu_out(1, 0, a, a + 2)
+            relu_out(1, 1, a, a + 2)
+            z_noise(1, a, a + 2)
+            z_out(1, a, a + 2)

@@ -23,7 +23,6 @@ FLOPS = 2 * TOKENS * IMAGE * HIDDEN + 2 * TOKENS * HIDDEN * 2 * LATENT
 GROUPS = 8
 HALF = 512
 ROWS = TOKENS // P
-SCALAR_PIECES = 2
 
 UNITS = [(0, 0)] + [(h, g - h) for g in range(1, GROUPS) for h in range(2)] + [(1, GROUPS - 1)]
 
@@ -68,22 +67,24 @@ def tile_mae_pa_kernel(tc, x_bytes, x_scale, eps, W11, b11, W31, b31, W32, b32, 
                 out=w_raw[pair][:, c, :, a:b], in_=w_view[c, :, :, 1024 * pair + a : 1024 * pair + b]
             )
 
-        w3_raw = [keep.tile([P, GROUPS, 512], BF16, name=f"w3_raw{i}") for i in range(2)]
+        w3_raw = keep.tile([P, 2, GROUPS, 512], BF16, name="w3_raw")
         w3_view = [w.rearrange("(g p j) l -> p g (j l)", p=P, j=4) for w in (W31, W32)]
 
         def load_w3(a, b):
             for i in range(2):
-                nc.sync.dma_start(out=w3_raw[i][:, a:b, :], in_=w3_view[i][:, a:b, :])
+                nc.sync.dma_start(out=w3_raw[:, i, a:b, :], in_=w3_view[i][:, a:b, :])
 
-        load_x(0, 0, 2)
+        load_x(0, 0, 1)
+        load_w(0, 0, 0, 256)
+        load_x(0, 1, 2)
+        load_w(0, 0, 256, 512)
         load_x(0, 2, 4)
-        load_w(0, 0, 0, 512)
         load_w(0, 1, 0, 512)
         bias_raw = keep.tile([P, GROUPS, 4], BF16, name="bias_raw")
         nc.scalar.dma_start(out=bias_raw[:], in_=b11.rearrange("(g p t) -> p g t", p=P, t=4))
-        load_x(1, 0, 4)
         load_w(0, 0, 512, 1024)
         load_w(0, 1, 512, 1024)
+        load_x(1, 0, 4)
         load_w3(0, 2)
         load_w(1, 0, 0, 1024)
         load_w(1, 1, 0, 1024)
@@ -122,7 +123,7 @@ def tile_mae_pa_kernel(tc, x_bytes, x_scale, eps, W11, b11, W31, b31, W32, b32, 
 
         def x_out(h, r):
             if xg[h] is None:
-                xg[h] = work.tile([P, 2, HALF, 4], BF16, name="xg", bufs=2, align_bytes=64)
+                xg[h] = work.tile([P, 2, HALF, 4], BF16, name="xg", bufs=1, align_bytes=64)
             dst = xg[h][:].rearrange("p c n t -> p (c n t)").bitcast(F32)
             dst = dst.rearrange("p (c n u) -> p c n u", c=2, u=2)
             nc.scalar.copy(
@@ -139,27 +140,29 @@ def tile_mae_pa_kernel(tc, x_bytes, x_scale, eps, W11, b11, W31, b31, W32, b32, 
 
         wg, w_codes, w_planes = {}, {}, {}
 
-        def w_piece(engine_copy, g, c, m):
-            if (g, c) not in wg:
-                wg[g, c] = work.tile([P, 2048], BF16, name="wg", bufs=4, align_bytes=64)
-            off = 512 * (g % 2) + 128 * m
+        def w_piece(engine_copy, g, c, a, b):
+            if g not in wg:
+                wg[g] = work.tile([P, 2, 2048], BF16, name="wg", bufs=3, align_bytes=64)
+            off = 512 * (g % 2)
+            src = w_raw[g // 2][:, c, :, off + 4 * a : off + 4 * b]
+            dst = wg[g][:, c, :].rearrange("p (t m i j) -> p m t j i", t=4, i=2, j=4)
             engine_copy(
-                out=wg[g, c][:].rearrange("p (t m j) -> p m j t", t=4, j=4)[:, 32 * m : 32 * (m + 1), :, :],
-                in_=w_raw[g // 2][:, c, :, off : off + 128].rearrange("p j (m t) -> p m j t", t=4),
+                out=dst[:, a // 2 : b // 2, :, :, :],
+                in_=src.rearrange("p j (m i t) -> p m t j i", t=4, i=2),
             )
 
-        def w_scalar(g, c, m):
-            w_piece(nc.scalar.copy, g, c, m)
+        def w_scalar(g, c, a, b):
+            w_piece(nc.scalar.copy, g, c, a, b)
 
-        def w_vector(g, c, m):
-            w_piece(nc.vector.tensor_copy, g, c, m)
+        def w_vector(g, c, a, b):
+            w_piece(nc.vector.tensor_copy, g, c, a, b)
 
         def w_quant(g, c):
             if g not in w_codes:
                 w_codes[g] = work.tile([P, 2, 512], U32, name="w_codes", bufs=4, align_bytes=64)
                 w_planes[g] = work.tile([P, 2, 512], U8, name="w_planes", bufs=4, align_bytes=64)
             nc.vector.quantize_mx(
-                out=w_codes[g][:, c, :].bitcast(FP8X4), scales=w_planes[g][:, c, :], in_=wg[g, c][:]
+                out=w_codes[g][:, c, :].bitcast(FP8X4), scales=w_planes[g][:, c, :], in_=wg[g][:, c, :]
             )
 
         w3g = {}
@@ -168,11 +171,10 @@ def tile_mae_pa_kernel(tc, x_bytes, x_scale, eps, W11, b11, W31, b31, W32, b32, 
 
         def w3_lay(g):
             w3g[g] = work.tile([P, 1024], BF16, name="w3g", bufs=2, align_bytes=64)
-            for i in range(2):
-                nc.vector.tensor_copy(
-                    out=w3g[g][:, 512 * i : 512 * (i + 1)].rearrange("p (c i j) -> p c j i", i=4, j=4),
-                    in_=w3_raw[i][:, g, :].rearrange("p (j c i) -> p c j i", j=4, i=4),
-                )
+            nc.vector.tensor_copy(
+                out=w3g[g][:].rearrange("p (w c i j) -> p w c j i", w=2, i=4, j=4),
+                in_=w3_raw[:, :, g, :].rearrange("p w (j c i) -> p w c j i", j=4, i=4),
+            )
 
         def w3_quant(g):
             nc.vector.quantize_mx(
@@ -182,25 +184,25 @@ def tile_mae_pa_kernel(tc, x_bytes, x_scale, eps, W11, b11, W31, b31, W32, b32, 
         bias = keep.tile([P, GROUPS, 4], F32, name="bias")
         enc, encg, enc_codes, enc_planes = {}, {}, {}, {}
 
-        def first_stage(h, g, between):
-            enc[h, g] = work.tile([P, 4, HALF], BF16, name="enc", bufs=3)
+        def first_stage(h, g, between, a=0, b=HALF):
+            if (h, g) not in enc:
+                enc[h, g] = work.tile([P, 4, HALF], BF16, name="enc", bufs=3)
             for t in range(4):
                 bank = psum.tile([P, 4, P], F32, name="bank")
-                flat = bank[:].rearrange("p a b -> p (a b)")
+                flat = bank[:].rearrange("p a b -> p (a b)")[:, : b - a]
                 for c in range(2):
                     nc.tensor.matmul_mx(
                         out=flat,
                         lhsT=w_codes[g][:, c, P * t : P * (t + 1)].bitcast(FP8X4),
                         lhsT_scale=w_planes[g][:, c, P * t : P * (t + 1)],
-                        rhs=x_codes[h][:, c, :].bitcast(FP8X4),
-                        rhs_scale=x_planes[h][:, c, :],
+                        rhs=x_codes[h][:, c, a:b].bitcast(FP8X4),
+                        rhs_scale=x_planes[h][:, c, a:b],
                         start=(c == 0),
                         stop=(c == 1),
                     )
-                nc.scalar.activation(out=enc[h, g][:, t, :], in_=flat, func=RELU, bias=bias[:, g, t : t + 1])
-                for call in between[t : t + 1]:
-                    for args in call:
-                        w_scalar(*args)
+                nc.scalar.activation(out=enc[h, g][:, t, a:b], in_=flat, func=RELU, bias=bias[:, g, t : t + 1])
+                for args in between.get(t, []):
+                    w_scalar(*args)
 
         def enc_lay(h, g, a=0, b=HALF):
             if (h, g) not in encg:
@@ -266,106 +268,94 @@ def tile_mae_pa_kernel(tc, x_bytes, x_scale, eps, W11, b11, W31, b31, W32, b32, 
             )
             nc.sync.dma_start(out=views[2][:, 4 * h + a : 4 * h + b, :], in_=z[h][:, a:b, :])
 
-        for r in range(4):
-            x_product(0, r)
-            x_turn(0, r)
-            x_out(0, r)
-            w_scalar(0, 0, r)
-        w_scalar(0, 1, 0)
+        def x_chain(h, r):
+            x_product(h, r)
+            x_turn(h, r)
+            x_out(h, r)
+
+        x_product(0, 0)
+        x_turn(0, 0)
+        w_scalar(0, 0, 0, 64)
+        x_out(0, 0)
+        x_chain(0, 1)
+        w_scalar(0, 0, 64, 128)
+        x_chain(0, 2)
+        x_chain(0, 3)
         nc.vector.tensor_copy(out=bias[:], in_=bias_raw[:])
-        for m in (1, 2, 3):
-            w_vector(0, 1, m)
+        w_vector(0, 1, 0, 64)
+        w_vector(0, 1, 64, 128)
         x_quant(0, 0)
         x_quant(0, 1)
         w_quant(0, 0)
         w_quant(0, 1)
-        w_scalar(1, 0, 0)
-        w_scalar(1, 0, 1)
+        for c in range(2):
+            for a in (0, 64):
+                w_scalar(1, c, a, a + 64)
 
-        first_stage(0, 0, [[(1, 0, 2)], [(1, 0, 3)], [(1, 1, 0)], [(1, 1, 1)]])
-        x_product(1, 0)
-        x_turn(1, 0)
-        x_out(1, 0)
-        x_product(1, 1)
-        x_turn(1, 1)
-        x_out(1, 1)
-        w_scalar(1, 1, 2)
-        w_scalar(1, 1, 3)
-        w3_lay(0)
-        enc_lay(0, 0)
-        x_product(1, 2)
-        x_turn(1, 2)
-        x_out(1, 2)
+        first_stage(0, 0, {3: [(2, 0, 0, 64)]})
+        x_chain(1, 0)
+        x_chain(1, 1)
         w_quant(1, 0)
-        enc_quant(0, 0)
-        x_product(1, 3)
-        x_turn(1, 3)
-        x_out(1, 3)
-        w3_quant(0)
+        x_chain(1, 2)
         w_quant(1, 1)
+        x_chain(1, 3)
+        enc_lay(0, 0)
+        w3_lay(0)
+        enc_quant(0, 0)
+        w3_quant(0)
 
-        first_stage(0, 1, [[(2, 0, 0)], [(2, 0, 1)], [(2, 1, 0)], [(2, 1, 1)]])
-        second_stage(0, 0)
-        w_vector(2, 0, 2)
-        w_vector(2, 0, 3)
+        first_stage(0, 1, {1: [(2, 1, 0, 64)]})
+        w_vector(2, 0, 64, 128)
         x_quant(1, 0)
         x_quant(1, 1)
-        w3_lay(1)
-        enc_lay(0, 1)
-        w_vector(2, 1, 2)
-        w_vector(2, 1, 3)
-        w3_quant(1)
-        enc_quant(0, 1)
         w_quant(2, 0)
+        w_vector(2, 1, 64, 128)
+        w3_lay(1)
 
         load_w(3, 0, 0, 1024)
         load_w(3, 1, 0, 1024)
 
         for step in range(2, 16):
             h, g = UNITS[step]
+            lh, lg = UNITS[step - 1]
             pg, pc = (step + 4) // 2, step % 2
             prep = pg < GROUPS
-            scalar_calls = [[], [], [], []]
-            if prep:
-                for m in range(SCALAR_PIECES):
-                    scalar_calls[2 * m + 1 if SCALAR_PIECES == 2 else m].append((pg, pc, m))
-            first_stage(h, g, scalar_calls)
-            ph, pgrp = UNITS[step - 1]
-            if ph == 0:
-                second_stage(ph, pgrp)
-            if step == 15:
-                for gg in range(GROUPS - 1):
-                    second_stage(1, gg)
-                z_noise(0, 0, 4)
-                z_out(0, 0, 4)
-                relu_out(0, 0, 0, 4)
-                relu_out(0, 1, 0, 4)
-                enc_lay(h, g, 0, 256)
-                enc_lay(h, g, 256, 512)
-                enc_quant(h, g, 0, 256)
-                enc_quant(h, g, 256, 512)
-                break
+            if step < 15:
+                first_stage(h, g, {1: [(pg, pc, 0, 64)]} if prep else {})
+            else:
+                first_stage(h, g, {}, 0, 256)
+                first_stage(h, g, {}, 256, 512)
             qg, qc = (step + 3) // 2, (step - 1) % 2
             if qg < GROUPS:
                 w_quant(qg, qc)
             if prep:
-                for m in range(SCALAR_PIECES, 4):
-                    w_vector(pg, pc, m)
-            w3_group = (step + 2) // 2 if step % 2 == 0 else (step + 1) // 2
-            enc_lay(h, g)
+                w_vector(pg, pc, 64, 128)
+            enc_lay(lh, lg)
+            w3_group = (step + 1) // 2
             if w3_group < GROUPS:
-                if step % 2 == 0:
+                if step % 2 == 1:
                     w3_lay(w3_group)
                 else:
-                    w3_quant(w3_group)
-            if step == 14:
-                add_bias(0, 0)
-                add_bias(0, 1)
-            enc_quant(h, g)
-            if step == 14:
-                add_bias(0, 2)
-                add_bias(0, 3)
+                    w3_quant(step // 2)
+            enc_quant(lh, lg)
+            sh, sg = UNITS[step - 2]
+            if sh == 0:
+                second_stage(sh, sg)
+            if step == 15:
+                for r in range(4):
+                    add_bias(0, r)
+                for gg in range(GROUPS - 1):
+                    second_stage(1, gg)
 
+        h, g = UNITS[15]
+        enc_lay(h, g, 0, 256)
+        z_noise(0, 0, 4)
+        enc_quant(h, g, 0, 256)
+        enc_lay(h, g, 256, 512)
+        z_out(0, 0, 4)
+        enc_quant(h, g, 256, 512)
+        relu_out(0, 0, 0, 4)
+        relu_out(0, 1, 0, 4)
         for a in (0, 2):
             second_stage(1, GROUPS - 1, rows=(a, a + 1))
         for a in (0, 2):

from contextlib import ExitStack

import concourse.mybir as mybir
from concourse.masks import make_identity

TOKENS, IMAGE, HIDDEN, LATENT = 1024, 1024, 4096, 128

F32 = mybir.dt.float32
BF16 = mybir.dt.bfloat16
U32 = mybir.dt.uint32
U8 = mybir.dt.uint8
FP8 = mybir.dt.float8_e4m3fn
FP8X4 = mybir.dt.float8_e4m3fn_x4

ADD = mybir.AluOpType.add
MULT = mybir.AluOpType.mult
MAX = mybir.AluOpType.max
RELU = mybir.ActivationFunctionType.Relu

P = 128
FLOPS = 2 * TOKENS * IMAGE * HIDDEN + 2 * TOKENS * HIDDEN * 2 * LATENT

GROUPS = 8
HALF = 512
ROWS = TOKENS // P

UNITS = [(0, 0)] + [(h, g - h) for g in range(1, GROUPS) for h in range(2)] + [(1, GROUPS - 1)]


def tile_mae_pa_kernel(tc, x_bytes, x_scale, eps, W11, b11, W31, b31, W32, b32, out_0, out_1, out_2):
    nc = tc.nc
    with ExitStack() as ctx:
        keep = ctx.enter_context(tc.tile_pool(name="keep", bufs=1))
        work = ctx.enter_context(tc.tile_pool(name="work", bufs=2))
        psum = ctx.enter_context(tc.psum_pool(name="psum", bufs=4))
        accs = ctx.enter_context(tc.psum_pool(name="accs", bufs=1))

        ident = keep.tile([P, P], F32, name="ident")
        make_identity(nc, ident[:])
        ctx.enter_context(tc.manual_schedule())
        ctx.enter_context(nc.allow_non_contiguous_dma(reason="runs of four biases"))

        warm = keep.tile([P, 1], F32, name="warm")
        nc.vector.memset(warm[:], 0.0)
        warm_out = keep.tile([P, 1], F32, name="warm_out")

        scale = keep.tile([P, IMAGE], F32, name="scale")
        nc.scalar.dma_start(out=scale[:], in_=x_scale.rearrange("o k -> (o k)").partition_broadcast(P))
        nc.scalar.activation(out=warm_out[:], in_=warm[:], func=RELU)

        xq = [keep.tile([P, 4 * IMAGE], U8, name=f"xq{h}") for h in range(2)]
        x_view = x_bytes.rearrange("(p r) k -> p (r k)", r=ROWS)

        def load_x(h, a, b):
            nc.sync.dma_start(
                out=xq[h][:, a * IMAGE : b * IMAGE],
                in_=x_view[:, (4 * h + a) * IMAGE : (4 * h + b) * IMAGE],
            )

        w_raw = [None] * 4
        w_view = W11.rearrange("(c p j) n -> c p j n", c=2, j=4)

        def load_w(pair, c, a, b):
            if w_raw[pair] is None:
                w_raw[pair] = work.tile([P, 2, 4, 1024], BF16, name="w_raw", bufs=3)
            nc.sync.dma_start(
                out=w_raw[pair][:, c, :, a:b], in_=w_view[c, :, :, 1024 * pair + a : 1024 * pair + b]
            )

        w3_raw = keep.tile([P, 2, GROUPS, 512], BF16, name="w3_raw")
        w3_view = [w.rearrange("(g p j) l -> p g (j l)", p=P, j=4) for w in (W31, W32)]

        def load_w3(a, b):
            for i in range(2):
                nc.sync.dma_start(out=w3_raw[:, i, a:b, :], in_=w3_view[i][:, a:b, :])

        load_x(0, 0, 1)
        load_w(0, 0, 0, 256)
        load_x(0, 1, 2)
        load_w(0, 0, 256, 512)
        load_x(0, 2, 4)
        load_w(0, 1, 0, 512)
        bias_raw = keep.tile([P, GROUPS, 4], BF16, name="bias_raw")
        nc.scalar.dma_start(out=bias_raw[:], in_=b11.rearrange("(g p t) -> p g t", p=P, t=4))
        load_w(0, 0, 512, 1024)
        load_w(0, 1, 512, 1024)
        load_x(1, 0, 4)
        load_w3(0, 2)
        load_w(1, 0, 0, 1024)
        load_w(1, 1, 0, 1024)
        load_w3(2, 8)
        bias3 = keep.tile([P, 2 * LATENT], BF16, name="bias3")
        nc.sync.dma_start(out=bias3[:, :LATENT], in_=b31.partition_broadcast(P))
        nc.sync.dma_start(out=bias3[:, LATENT:], in_=b32.partition_broadcast(P))
        eps_sb = keep.tile([P, ROWS, LATENT], BF16, name="eps_sb")
        nc.sync.dma_start(out=eps_sb[:], in_=eps.rearrange("(p r) l -> p r l", r=ROWS))
        load_w(2, 0, 0, 1024)
        load_w(2, 1, 0, 1024)

        xg = [None, None]
        x_codes = [keep.tile([P, 2, HALF], U32, name=f"x_codes{h}", align_bytes=64) for h in range(2)]
        x_planes = [keep.tile([P, 2, HALF], U8, name=f"x_planes{h}", align_bytes=64) for h in range(2)]

        xb = {}

        def x_product(h, r):
            xb[h, r] = work.tile([P, IMAGE], BF16, name="xb", bufs=3)
            nc.vector.tensor_tensor(
                out=xb[h, r][:], in0=xq[h][:, r * IMAGE : (r + 1) * IMAGE].bitcast(FP8), in1=scale[:], op=MULT
            )

        x_banks = {}

        def x_turn(h, r):
            bank = psum.tile([P, 4, P], F32, name="bank")
            words = xb[h, r][:].bitcast(F32)
            for c in range(2):
                for u in range(2):
                    nc.tensor.transpose(
                        bank[:, 2 * c + u, :], words[:, 256 * c + u : 256 * (c + 1) : 2], ident[:]
                    )
            x_banks[h, r] = bank

        def x_out(h, r):
            if xg[h] is None:
                xg[h] = work.tile([P, 2, HALF, 4], BF16, name="xg", bufs=1, align_bytes=64)
            dst = xg[h][:].rearrange("p c n t -> p (c n t)").bitcast(F32)
            dst = dst.rearrange("p (c n u) -> p c n u", c=2, u=2)
            nc.scalar.copy(
                out=dst[:, :, P * r : P * (r + 1), :],
                in_=x_banks[h, r][:].rearrange("p (c u) n -> p c n u", u=2),
            )

        def x_quant(h, c):
            nc.vector.quantize_mx(
                out=x_codes[h][:, c, :].bitcast(FP8X4),
                scales=x_planes[h][:, c, :],
                in_=xg[h][:, c, :, :].rearrange("p n t -> p (n t)"),
            )

        wg, w_codes, w_planes = {}, {}, {}

        def w_piece(engine_copy, g, c, a, b):
            if g not in wg:
                wg[g] = work.tile([P, 2, 2048], BF16, name="wg", bufs=3, align_bytes=64)
            off = 512 * (g % 2)
            src = w_raw[g // 2][:, c, :, off + 4 * a : off + 4 * b]
            dst = wg[g][:, c, :].rearrange("p (t m i j) -> p m t j i", t=4, i=2, j=4)
            engine_copy(
                out=dst[:, a // 2 : b // 2, :, :, :],
                in_=src.rearrange("p j (m i t) -> p m t j i", t=4, i=2),
            )

        def w_scalar(g, c, a, b):
            w_piece(nc.scalar.copy, g, c, a, b)

        def w_vector(g, c, a, b):
            w_piece(nc.vector.tensor_copy, g, c, a, b)

        def w_quant(g, c):
            if g not in w_codes:
                w_codes[g] = work.tile([P, 2, 512], U32, name="w_codes", bufs=4, align_bytes=64)
                w_planes[g] = work.tile([P, 2, 512], U8, name="w_planes", bufs=4, align_bytes=64)
            nc.vector.quantize_mx(
                out=w_codes[g][:, c, :].bitcast(FP8X4), scales=w_planes[g][:, c, :], in_=wg[g][:, c, :]
            )

        w3g = {}
        w3_codes = keep.tile([P, GROUPS, 2 * LATENT], U32, name="w3_codes", align_bytes=64)
        w3_planes = keep.tile([P, GROUPS, 2 * LATENT], U8, name="w3_planes", align_bytes=64)

        def w3_lay(g):
            w3g[g] = work.tile([P, 1024], BF16, name="w3g", bufs=2, align_bytes=64)
            nc.vector.tensor_copy(
                out=w3g[g][:].rearrange("p (w c i j) -> p w c j i", w=2, i=4, j=4),
                in_=w3_raw[:, :, g, :].rearrange("p w (j c i) -> p w c j i", j=4, i=4),
            )

        def w3_quant(g):
            nc.vector.quantize_mx(
                out=w3_codes[:, g, :].bitcast(FP8X4), scales=w3_planes[:, g, :], in_=w3g[g][:]
            )

        bias = keep.tile([P, GROUPS, 4], F32, name="bias")
        enc, encg, enc_codes, enc_planes = {}, {}, {}, {}

        def first_stage(h, g, between, a=0, b=HALF):
            if (h, g) not in enc:
                enc[h, g] = work.tile([P, 4, HALF], BF16, name="enc", bufs=3)
            for t in range(4):
                bank = psum.tile([P, 4, P], F32, name="bank")
                flat = bank[:].rearrange("p a b -> p (a b)")[:, : b - a]
                for c in range(2):
                    nc.tensor.matmul_mx(
                        out=flat,
                        lhsT=w_codes[g][:, c, P * t : P * (t + 1)].bitcast(FP8X4),
                        lhsT_scale=w_planes[g][:, c, P * t : P * (t + 1)],
                        rhs=x_codes[h][:, c, a:b].bitcast(FP8X4),
                        rhs_scale=x_planes[h][:, c, a:b],
                        start=(c == 0),
                        stop=(c == 1),
                    )
                nc.scalar.activation(out=enc[h, g][:, t, a:b], in_=flat, func=RELU, bias=bias[:, g, t : t + 1])
                for args in between.get(t, []):
                    w_scalar(*args)

        def enc_lay(h, g, a=0, b=HALF):
            if (h, g) not in encg:
                encg[h, g] = work.tile([P, 4 * HALF], BF16, name="encg", bufs=3, align_bytes=64)
            nc.vector.tensor_copy(
                out=encg[h, g][:, 4 * a : 4 * b].rearrange("p (c i t) -> p c t i", i=4, t=4),
                in_=enc[h, g][:, :, a:b].rearrange("p t (c i) -> p c t i", i=4),
            )

        def enc_quant(h, g, a=0, b=HALF):
            if (h, g) not in enc_codes:
                bufs = 3 if h == 0 else 8
                enc_codes[h, g] = work.tile([P, HALF], U32, name=f"enc_codes{h}", bufs=bufs, align_bytes=64)
                enc_planes[h, g] = work.tile([P, HALF], U8, name=f"enc_planes{h}", bufs=bufs, align_bytes=64)
            nc.vector.quantize_mx(
                out=enc_codes[h, g][:, a:b].bitcast(FP8X4),
                scales=enc_planes[h, g][:, a:b],
                in_=encg[h, g][:, 4 * a : 4 * b],
            )

        acc = {}

        def second_stage(h, g, rows=(0, 1, 2, 3)):
            for r in rows:
                if (h, r) not in acc:
                    acc[h, r] = accs.tile([P, 2 * LATENT], F32, name=f"acc{r}")
                nc.tensor.matmul_mx(
                    out=acc[h, r][:],
                    lhsT=enc_codes[h, g][:, P * r : P * (r + 1)].bitcast(FP8X4),
                    lhsT_scale=enc_planes[h, g][:, P * r : P * (r + 1)],
                    rhs=w3_codes[:, g, :].bitcast(FP8X4),
                    rhs_scale=w3_planes[:, g, :],
                    start=(g == 0),
                    stop=(g == GROUPS - 1),
                )

        y, z, relus = {}, {}, {}
        views = [o.rearrange("(p r) l -> p r l", r=ROWS) for o in (out_0, out_1, out_2)]

        def add_bias(h, r):
            if h not in y:
                y[h] = work.tile([P, 4, 2 * LATENT], F32, name="y", bufs=2)
                z[h] = work.tile([P, 4, LATENT], F32, name="z", bufs=2)
                relus[h] = [work.tile([P, 4, LATENT], F32, name=f"relu{i}", bufs=2) for i in range(2)]
            nc.vector.tensor_tensor(out=y[h][:, r, :], in0=acc[h, r][:], in1=bias3[:], op=ADD)

        def relu_out(h, i, a, b):
            nc.scalar.activation(
                out=relus[h][i][:, a:b, :], in_=y[h][:, a:b, LATENT * i : LATENT * (i + 1)], func=RELU
            )
            nc.sync.dma_start(out=views[i][:, 4 * h + a : 4 * h + b, :], in_=relus[h][i][:, a:b, :])

        def z_noise(h, a, b):
            nc.vector.scalar_tensor_tensor(
                out=z[h][:, a:b, :], in0=y[h][:, a:b, LATENT:], scalar=0.0,
                in1=eps_sb[:, 4 * h + a : 4 * h + b, :], op0=MAX, op1=MULT,
            )

        def z_out(h, a, b):
            nc.vector.scalar_tensor_tensor(
                out=z[h][:, a:b, :], in0=y[h][:, a:b, :LATENT], scalar=0.0,
                in1=z[h][:, a:b, :], op0=MAX, op1=ADD,
            )
            nc.sync.dma_start(out=views[2][:, 4 * h + a : 4 * h + b, :], in_=z[h][:, a:b, :])

        def x_chain(h, r):
            x_product(h, r)
            x_turn(h, r)
            x_out(h, r)

        x_product(0, 0)
        x_turn(0, 0)
        w_scalar(0, 0, 0, 64)
        x_out(0, 0)
        x_chain(0, 1)
        w_scalar(0, 0, 64, 128)
        x_chain(0, 2)
        x_chain(0, 3)
        nc.vector.tensor_copy(out=bias[:], in_=bias_raw[:])
        w_vector(0, 1, 0, 64)
        w_vector(0, 1, 64, 128)
        x_quant(0, 0)
        x_quant(0, 1)
        w_quant(0, 0)
        w_quant(0, 1)
        for c in range(2):
            for a in (0, 64):
                w_scalar(1, c, a, a + 64)

        first_stage(0, 0, {3: [(2, 0, 0, 64)]})
        x_chain(1, 0)
        x_chain(1, 1)
        w_quant(1, 0)
        x_chain(1, 2)
        w_quant(1, 1)
        x_chain(1, 3)
        enc_lay(0, 0)
        w3_lay(0)
        enc_quant(0, 0)
        w3_quant(0)

        first_stage(0, 1, {1: [(2, 1, 0, 64)]})
        w_vector(2, 0, 64, 128)
        x_quant(1, 0)
        x_quant(1, 1)
        w_quant(2, 0)
        w_vector(2, 1, 64, 128)
        w3_lay(1)

        load_w(3, 0, 0, 1024)
        load_w(3, 1, 0, 1024)

        for step in range(2, 16):
            h, g = UNITS[step]
            lh, lg = UNITS[step - 1]
            pg, pc = (step + 4) // 2, step % 2
            prep = pg < GROUPS
            if step < 15:
                first_stage(h, g, {1: [(pg, pc, 0, 64)]} if prep else {})
            else:
                first_stage(h, g, {}, 0, 256)
                first_stage(h, g, {}, 256, 512)
            qg, qc = (step + 3) // 2, (step - 1) % 2
            if qg < GROUPS:
                w_quant(qg, qc)
            if prep:
                w_vector(pg, pc, 64, 128)
            enc_lay(lh, lg)
            w3_group = (step + 1) // 2
            if w3_group < GROUPS:
                if step % 2 == 1:
                    w3_lay(w3_group)
                else:
                    w3_quant(step // 2)
            enc_quant(lh, lg)
            sh, sg = UNITS[step - 2]
            if sh == 0:
                second_stage(sh, sg)
            if step == 15:
                for r in range(4):
                    add_bias(0, r)
                for gg in range(GROUPS - 1):
                    second_stage(1, gg)

        h, g = UNITS[15]
        enc_lay(h, g, 0, 256)
        z_noise(0, 0, 4)
        enc_quant(h, g, 0, 256)
        enc_lay(h, g, 256, 512)
        z_out(0, 0, 4)
        enc_quant(h, g, 256, 512)
        relu_out(0, 0, 0, 4)
        relu_out(0, 1, 0, 4)
        for a in (0, 2):
            second_stage(1, GROUPS - 1, rows=(a, a + 1))
        for a in (0, 2):
            add_bias(1, a)
            add_bias(1, a + 1)
            relu_out(1, 0, a, a + 2)
            relu_out(1, 1, a, a + 2)
            z_noise(1, a, a + 2)
            z_out(1, a, a + 2)
